import numpy as np
import ml_dtypes

BF16 = ml_dtypes.bfloat16


def bf(x):
    return np.asarray(x, np.float32).astype(BF16)


def f32(x):
    return np.asarray(x, np.float32)


def f64(x):
    return np.asarray(x).astype(np.float64)


def striped(idx):
    return np.tile(idx.reshape(-1, 16).T, (8, 1))


C, S, N = 128, 512, 256
EPS = 1e-6
PE_BASE = 10000.0


def pos_table():
    pos = np.arange(N, dtype=np.float32)[:, None]
    div = np.exp(np.arange(C // 2, dtype=np.float32) * np.float32(-np.log(PE_BASE) / (C // 2 - 1)))
    return np.ascontiguousarray(np.concatenate([np.sin(pos * div), np.cos(pos * div)], axis=-1).T)


def setup_inputs():
    return {"emb": f32(np.random.standard_normal((C, S))), "pe": f32(pos_table()), "ln_w": f32(1.0 + 0.1 * np.random.standard_normal((C, 1))), "ln_b": f32(0.1 * np.random.standard_normal((C, 1))), "offs": striped(np.random.permutation(np.tile(np.arange(S), 2))[:N])}


def reference(emb, pe, ln_w, ln_b, offs):
    idx = offs[:16].T.reshape(-1)
    x = f64(emb)[:, idx] + f64(pe)
    m = x.mean(axis=0, keepdims=True)
    v = np.square(x - m).mean(axis=0, keepdims=True)
    h = (x - m) / np.sqrt(v + EPS) * f64(ln_w) + f64(ln_b)
    return np.concatenate([x, h], axis=0)

@@ -1,0 +1,89 @@
+import concourse.mybir as mybir
+from concourse.masks import make_identity
+
+F32 = mybir.dt.float32
+U16 = mybir.dt.uint16
+ALU = mybir.AluOpType
+ACT = mybir.ActivationFunctionType
+
+C, S, N = 128, 512, 256
+EPS = 1e-6
+PIECES = 2
+W = N // PIECES
+WARMING = 5
+FLOPS = 2 * C * C * N
+
+
+def tile_transformernet_kernel(tc, emb, pe, ln_w, ln_b, offs, out):
+    nc = tc.nc
+    with (
+        tc.tile_pool(name="held", bufs=1) as held,
+        tc.psum_pool(name="psum", bufs=1) as psum,
+    ):
+        table = held.tile([C, S], F32, name="table")
+        nc.scalar.dma_start(table[:], emb)
+        place = held.tile([C, N], F32, name="place")
+        nc.sync.dma_start(place[:], pe)
+        offsets = held.tile([C, N // 16], U16, name="offsets")
+        nc.sync.dma_start(offsets[:], offs)
+        gain = held.tile([C, 1], F32, name="gain")
+        nc.sync.dma_start(gain[:], ln_w)
+        shift = held.tile([C, 1], F32, name="shift")
+        nc.sync.dma_start(shift[:], ln_b)
+
+        centre = held.tile([C, C], F32, name="centre")
+        nc.gpsimd.memset(centre[:], -1.0 / C)
+        nc.gpsimd.affine_select(
+            out=centre[:],
+            in_=centre[:],
+            compare_op=ALU.not_equal,
+            fill=1.0 - 1.0 / C,
+            base=0,
+            pattern=[[-1, C]],
+            channel_multiplier=1,
+        )
+        identity = held.tile([W, W], F32, name="identity")
+        make_identity(nc, identity[:])
+        eps = held.tile([W, 1], F32, name="eps")
+        nc.vector.memset(eps[:], EPS)
+        ones = held.tile([C, C], F32, name="ones")
+        nc.vector.memset(ones[:], 1.0)
+        first_use = held.tile([C, 1], F32, name="first_use")
+        nc.scalar.activation(first_use[:], ones[:, 0:1], ACT.Abs_reciprocal_sqrt)
+        unread = psum.tile([C, C], F32, name="unread")
+        for _ in range(WARMING):
+            nc.tensor.matmul(unread[:], ones[:], ones[:], start=True, stop=True)
+
+        pieces = range(PIECES)
+        x = [held.tile([C, W], F32, name=f"x{p}") for p in pieces]
+        turned = [psum.tile([W, C], F32, name=f"turned{p}") for p in pieces]
+        scaled = [held.tile([W, C], F32, name=f"scaled{p}") for p in pieces]
+        squares = [held.tile([W, C], F32, name=f"squares{p}") for p in pieces]
+        variance = [held.tile([W, 1], F32, name=f"variance{p}") for p in pieces]
+        inverse = [held.tile([W, 1], F32, name=f"inverse{p}") for p in pieces]
+        normed = [psum.tile([C, W], F32, name=f"normed{p}") for p in pieces]
+        h = [held.tile([C, W], F32, name=f"h{p}") for p in pieces]
+
+        for p in pieces:
+            nc.vector.tensor_tensor(
+                x[p][:],
+                table[:].indirect(offsets[:, p * W // 16 : (p + 1) * W // 16]),
+                place[:, p * W : (p + 1) * W],
+                ALU.add,
+            )
+            nc.sync.dma_start(out[0:C, p * W : (p + 1) * W], x[p][:])
+
+        for p in pieces:
+            nc.tensor.matmul(turned[p][:], x[p][:], centre[:], start=True, stop=True)
+        for p in pieces:
+            nc.scalar.activation(
+                squares[p][:], turned[p][:], ACT.Square, scale=C**-0.5, accum_out=variance[p][:]
+            )
+            nc.scalar.activation(
+                inverse[p][:], variance[p][:], ACT.Abs_reciprocal_sqrt, bias=eps[:]
+            )
+            nc.vector.tensor_scalar_mul(scaled[p][:], turned[p][:], inverse[p][:])
+        for p in pieces:
+            nc.tensor.transpose(normed[p][:], scaled[p][:], identity[:])
+            nc.vector.tensor_scalar(h[p][:], normed[p][:], gain[:], shift[:], ALU.mult, ALU.add)
+            nc.sync.dma_start(out[C : 2 * C, p * W : (p + 1) * W], h[p][:])

@@ -26,10 +26,6 @@ def tile_transformernet_kernel(tc, emb, pe, ln_w, ln_b, offs, out):
         nc.sync.dma_start(place[:], pe)
         offsets = held.tile([C, N // 16], U16, name="offsets")
         nc.sync.dma_start(offsets[:], offs)
-        gain = held.tile([C, 1], F32, name="gain")
-        nc.sync.dma_start(gain[:], ln_w)
-        shift = held.tile([C, 1], F32, name="shift")
-        nc.sync.dma_start(shift[:], ln_b)
 
         centre = held.tile([C, C], F32, name="centre")
         nc.gpsimd.memset(centre[:], -1.0 / C)
@@ -44,6 +40,10 @@ def tile_transformernet_kernel(tc, emb, pe, ln_w, ln_b, offs, out):
         )
         identity = held.tile([W, W], F32, name="identity")
         make_identity(nc, identity[:])
+        gain = held.tile([C, 1], F32, name="gain")
+        nc.gpsimd.dma_start(gain[:], ln_w)
+        shift = held.tile([C, 1], F32, name="shift")
+        nc.gpsimd.dma_start(shift[:], ln_b)
         eps = held.tile([W, 1], F32, name="eps")
         nc.vector.memset(eps[:], EPS)
         ones = held.tile([C, C], F32, name="ones")

@@ -11,7 +11,6 @@ EPS = 1e-6
 PIECES = 2
 W = N // PIECES
 WARMING = 5
-FLOPS = 2 * C * C * N
 
 
 def tile_transformernet_kernel(tc, emb, pe, ln_w, ln_b, offs, out):
@@ -27,17 +26,6 @@ def tile_transformernet_kernel(tc, emb, pe, ln_w, ln_b, offs, out):
         offsets = held.tile([C, N // 16], U16, name="offsets")
         nc.sync.dma_start(offsets[:], offs)
 
-        centre = held.tile([C, C], F32, name="centre")
-        nc.gpsimd.memset(centre[:], -1.0 / C)
-        nc.gpsimd.affine_select(
-            out=centre[:],
-            in_=centre[:],
-            compare_op=ALU.not_equal,
-            fill=1.0 - 1.0 / C,
-            base=0,
-            pattern=[[-1, C]],
-            channel_multiplier=1,
-        )
         identity = held.tile([W, W], F32, name="identity")
         make_identity(nc, identity[:])
         gain = held.tile([C, 1], F32, name="gain")
@@ -57,10 +45,9 @@ def tile_transformernet_kernel(tc, emb, pe, ln_w, ln_b, offs, out):
         pieces = range(PIECES)
         x = [held.tile([C, W], F32, name=f"x{p}") for p in pieces]
         turned = [psum.tile([W, C], F32, name=f"turned{p}") for p in pieces]
-        scaled = [held.tile([W, C], F32, name=f"scaled{p}") for p in pieces]
-        squares = [held.tile([W, C], F32, name=f"squares{p}") for p in pieces]
-        variance = [held.tile([W, 1], F32, name=f"variance{p}") for p in pieces]
+        stats = [held.tile([W, 6], F32, name=f"stats{p}") for p in pieces]
         inverse = [held.tile([W, 1], F32, name=f"inverse{p}") for p in pieces]
+        scaled = [held.tile([W, C], F32, name=f"scaled{p}") for p in pieces]
         normed = [psum.tile([C, W], F32, name=f"normed{p}") for p in pieces]
         h = [held.tile([C, W], F32, name=f"h{p}") for p in pieces]
 
@@ -74,15 +61,17 @@ def tile_transformernet_kernel(tc, emb, pe, ln_w, ln_b, offs, out):
             nc.sync.dma_start(out[0:C, p * W : (p + 1) * W], x[p][:])
 
         for p in pieces:
-            nc.tensor.matmul(turned[p][:], x[p][:], centre[:], start=True, stop=True)
+            nc.tensor.transpose(turned[p][:], x[p][:], identity[:])
+            nc.vector.bn_stats(stats[p][:], turned[p][:].unsqueeze(2).to_broadcast([W, C, 2]))
+        mean = [stats[p][:, 1:2] for p in pieces]
+        sum_squares = [stats[p][:, 2:3] for p in pieces]
         for p in pieces:
             nc.scalar.activation(
-                squares[p][:], turned[p][:], ACT.Square, scale=C**-0.5, accum_out=variance[p][:]
+                inverse[p][:], sum_squares[p], ACT.Abs_reciprocal_sqrt, bias=eps[:], scale=1.0 / C
             )
-            nc.scalar.activation(
-                inverse[p][:], variance[p][:], ACT.Abs_reciprocal_sqrt, bias=eps[:]
+            nc.vector.tensor_scalar(
+                scaled[p][:], turned[p][:], mean[p], inverse[p][:], ALU.subtract, ALU.mult
             )
-            nc.vector.tensor_scalar_mul(scaled[p][:], turned[p][:], inverse[p][:])
         for p in pieces:
             nc.tensor.transpose(normed[p][:], scaled[p][:], identity[:])
             nc.vector.tensor_scalar(h[p][:], normed[p][:], gain[:], shift[:], ALU.mult, ALU.add)

@@ -43,7 +43,7 @@ def tile_transformernet_kernel(tc, emb, pe, ln_w, ln_b, offs, out):
             nc.tensor.matmul(unread[:], ones[:], ones[:], start=True, stop=True)
 
         pieces = range(PIECES)
-        x = [held.tile([C, W], F32, name=f"x{p}") for p in pieces]
+        x = held.tile([C, N], F32, name="x")
         turned = [psum.tile([W, C], F32, name=f"turned{p}") for p in pieces]
         stats = [held.tile([W, 6], F32, name=f"stats{p}") for p in pieces]
         inverse = [held.tile([W, 1], F32, name=f"inverse{p}") for p in pieces]
@@ -53,15 +53,15 @@ def tile_transformernet_kernel(tc, emb, pe, ln_w, ln_b, offs, out):
 
         for p in pieces:
             nc.vector.tensor_tensor(
-                x[p][:],
+                x[:, p * W : (p + 1) * W],
                 table[:].indirect(offsets[:, p * W // 16 : (p + 1) * W // 16]),
                 place[:, p * W : (p + 1) * W],
                 ALU.add,
             )
-            nc.sync.dma_start(out[0:C, p * W : (p + 1) * W], x[p][:])
+        nc.sync.dma_start(out[0:C, :], x[:])
 
         for p in pieces:
-            nc.tensor.transpose(turned[p][:], x[p][:], identity[:])
+            nc.tensor.transpose(turned[p][:], x[:, p * W : (p + 1) * W], identity[:])
             nc.vector.bn_stats(stats[p][:], turned[p][:].unsqueeze(2).to_broadcast([W, C, 2]))
         mean = [stats[p][:, 1:2] for p in pieces]
         sum_squares = [stats[p][:, 2:3] for p in pieces]

@@ -25,13 +25,13 @@ def tile_transformernet_kernel(tc, emb, pe, ln_w, ln_b, offs, out):
         nc.sync.dma_start(place[:], pe)
         offsets = held.tile([C, N // 16], U16, name="offsets")
         nc.sync.dma_start(offsets[:], offs)
+        gain = held.tile([C, 1], F32, name="gain")
+        nc.sync.dma_start(gain[:], ln_w)
+        shift = held.tile([C, 1], F32, name="shift")
+        nc.sync.dma_start(shift[:], ln_b)
 
         identity = held.tile([W, W], F32, name="identity")
         make_identity(nc, identity[:])
-        gain = held.tile([C, 1], F32, name="gain")
-        nc.gpsimd.dma_start(gain[:], ln_w)
-        shift = held.tile([C, 1], F32, name="shift")
-        nc.gpsimd.dma_start(shift[:], ln_b)
         eps = held.tile([W, 1], F32, name="eps")
         nc.vector.memset(eps[:], EPS)
         ones = held.tile([C, C], F32, name="ones")

@@ -58,7 +58,7 @@ def tile_transformernet_kernel(tc, emb, pe, ln_w, ln_b, offs, out):
                 place[:, p * W : (p + 1) * W],
                 ALU.add,
             )
-        nc.sync.dma_start(out[0:C, :], x[:])
+        nc.scalar.dma_start(out[0:C, :], x[:])
 
         for p in pieces:
             nc.tensor.transpose(turned[p][:], x[:, p * W : (p + 1) * W], identity[:])

import concourse.mybir as mybir
from concourse.masks import make_identity

F32 = mybir.dt.float32
U16 = mybir.dt.uint16
ALU = mybir.AluOpType
ACT = mybir.ActivationFunctionType

C, S, N = 128, 512, 256
EPS = 1e-6
PIECES = 2
W = N // PIECES
WARMING = 5


def tile_transformernet_kernel(tc, emb, pe, ln_w, ln_b, offs, out):
    nc = tc.nc
    with (
        tc.tile_pool(name="held", bufs=1) as held,
        tc.psum_pool(name="psum", bufs=1) as psum,
    ):
        table = held.tile([C, S], F32, name="table")
        nc.scalar.dma_start(table[:], emb)
        place = held.tile([C, N], F32, name="place")
        nc.sync.dma_start(place[:], pe)
        offsets = held.tile([C, N // 16], U16, name="offsets")
        nc.sync.dma_start(offsets[:], offs)
        gain = held.tile([C, 1], F32, name="gain")
        nc.sync.dma_start(gain[:], ln_w)
        shift = held.tile([C, 1], F32, name="shift")
        nc.sync.dma_start(shift[:], ln_b)

        identity = held.tile([W, W], F32, name="identity")
        make_identity(nc, identity[:])
        eps = held.tile([W, 1], F32, name="eps")
        nc.vector.memset(eps[:], EPS)
        ones = held.tile([C, C], F32, name="ones")
        nc.vector.memset(ones[:], 1.0)
        first_use = held.tile([C, 1], F32, name="first_use")
        nc.scalar.activation(first_use[:], ones[:, 0:1], ACT.Abs_reciprocal_sqrt)
        unread = psum.tile([C, C], F32, name="unread")
        for _ in range(WARMING):
            nc.tensor.matmul(unread[:], ones[:], ones[:], start=True, stop=True)

        pieces = range(PIECES)
        x = held.tile([C, N], F32, name="x")
        turned = [psum.tile([W, C], F32, name=f"turned{p}") for p in pieces]
        stats = [held.tile([W, 6], F32, name=f"stats{p}") for p in pieces]
        inverse = [held.tile([W, 1], F32, name=f"inverse{p}") for p in pieces]
        scaled = [held.tile([W, C], F32, name=f"scaled{p}") for p in pieces]
        normed = [psum.tile([C, W], F32, name=f"normed{p}") for p in pieces]
        h = [held.tile([C, W], F32, name=f"h{p}") for p in pieces]

        for p in pieces:
            nc.vector.tensor_tensor(
                x[:, p * W : (p + 1) * W],
                table[:].indirect(offsets[:, p * W // 16 : (p + 1) * W // 16]),
                place[:, p * W : (p + 1) * W],
                ALU.add,
            )
        nc.scalar.dma_start(out[0:C, :], x[:])

        for p in pieces:
            nc.tensor.transpose(turned[p][:], x[:, p * W : (p + 1) * W], identity[:])
            nc.vector.bn_stats(stats[p][:], turned[p][:].unsqueeze(2).to_broadcast([W, C, 2]))
        mean = [stats[p][:, 1:2] for p in pieces]
        sum_squares = [stats[p][:, 2:3] for p in pieces]
        for p in pieces:
            nc.scalar.activation(
                inverse[p][:], sum_squares[p], ACT.Abs_reciprocal_sqrt, bias=eps[:], scale=1.0 / C
            )
            nc.vector.tensor_scalar(
                scaled[p][:], turned[p][:], mean[p], inverse[p][:], ALU.subtract, ALU.mult
            )
        for p in pieces:
            nc.tensor.transpose(normed[p][:], scaled[p][:], identity[:])
            nc.vector.tensor_scalar(h[p][:], normed[p][:], gain[:], shift[:], ALU.mult, ALU.add)
            nc.sync.dma_start(out[C : 2 * C, p * W : (p + 1) * W], h[p][:])
